import numpy as np
import ml_dtypes


def mxq(x, axis, fmt="e4m3"):
    dtype, down = {"e4m3": (ml_dtypes.float8_e4m3fn, 7), "e5m2": (ml_dtypes.float8_e5m2, 14)}[fmt]
    v = np.moveaxis(np.asarray(x, np.float32).astype(ml_dtypes.bfloat16).astype(np.float64), axis, -1)
    blocks = v.reshape(v.shape[:-1] + (-1, 32))
    amax = np.abs(blocks).max(-1, keepdims=True)
    byte = np.maximum(np.where(amax > 0, np.frexp(amax)[1] - 1 + 127, 0) - down, 1)
    scale = np.exp2(byte - 127.0)
    codes = (blocks / scale).astype(np.float32).astype(dtype).astype(np.float64)
    return np.moveaxis((codes * scale).reshape(v.shape), -1, axis)


WIDE = False


def mx_kscale(k):
    if not WIDE:
        return np.ones(k)
    levels = np.array([10, -10, 5, -5, 0])
    a = np.random.permutation(np.resize(levels, k // 512 * 4)).reshape(k // 512, 4)
    idx = np.arange(k)
    return np.exp2(a[idx // 512, idx % 128 // 32])


BF16 = ml_dtypes.bfloat16


def bf(x):
    return np.asarray(x, np.float32).astype(BF16)


def f64(x):
    return np.asarray(x).astype(np.float64)


B, CI, C, VI, V, N, M = 3, 512, 512, 512, 512, 768, 1024
EPS = 1e-5
QS = np.sqrt(2.0) / C ** 0.25


def instance_norm(x):
    mu = x.mean(-1, keepdims=True)
    var = np.square(x - mu).mean(-1, keepdims=True)
    return (x - mu) * (1.0 / np.sqrt(var + EPS))


def norm_rms(a):
    return a / np.sqrt(a * a + EPS)


def setup_inputs():
    k = mx_kscale(CI)
    t = (k / k.max())[:, None]
    g = np.exp2(np.random.uniform(-8.0, 1.0, (CI, 1)))
    d = np.exp2(np.round(np.log2(norm_rms(g * t) / norm_rms(g))))[:, 0]
    q = g * t * (np.random.standard_normal((B, CI, N)) + 0.5 * np.random.standard_normal((B, CI, 1)))
    return {"q": bf(q), "Wq": bf(np.random.standard_normal((C, CI)) * QS / np.sqrt(CI) / d[None, :]), "bq": bf(np.random.standard_normal(C) * 0.3 * QS)}


def reference(q, Wq, bq):
    xn = instance_norm(f64(q))
    return (mxq(f64(Wq), 1, "e4m3") @ mxq(xn, 1, "e4m3")) + f64(bq)[None, :, None]

@@ -1,0 +1,156 @@
+from contextlib import ExitStack
+
+import concourse.mybir as mybir
+from concourse.masks import make_identity
+
+F32 = mybir.dt.float32
+BF16 = mybir.dt.bfloat16
+U32 = mybir.dt.uint32
+U8 = mybir.dt.uint8
+FP8X4 = mybir.dt.float8_e4m3fn_x4
+ALU = mybir.AluOpType
+ACT = mybir.ActivationFunctionType
+
+P = 128
+PACK = 4
+BATCH = 3
+CHANNELS = P * PACK
+POSITIONS = 768
+EPS = 1e-5
+STAT_PIECES = 2
+STAT_DIM = 6
+WIDE = (0, 512)
+NARROW = (512, 256)
+BANK = 512
+
+FLOPS = 2 * BATCH * CHANNELS * CHANNELS * POSITIONS
+
+
+def tile_adaattn3dstylizer_pa_kernel(tc, q, Wq, bq, out):
+    nc = tc.nc
+    with ExitStack() as ctx:
+        const = ctx.enter_context(tc.tile_pool(name="const", bufs=1))
+        batch_pool = ctx.enter_context(tc.tile_pool(name="batch", bufs=BATCH))
+        psum_setup = ctx.enter_context(tc.psum_pool(name="psum_setup", bufs=2))
+        psum_acc = ctx.enter_context(tc.psum_pool(name="psum_acc", bufs=6))
+
+        table_warmer = const.tile([P, 1], F32)
+        nc.vector.memset(table_warmer[:], 1.0)
+        nc.scalar.activation(out=table_warmer[:], in_=table_warmer[:], func=ACT.Sqrt)
+        identity = const.tile([P, P], F32)
+        make_identity(nc, identity[:])
+
+        q_rows = []
+        for b in range(BATCH):
+            q_sb = batch_pool.tile([P, PACK, POSITIONS], BF16)
+            q_rows.append(q_sb)
+        w_sb = const.tile([P, PACK, CHANNELS], BF16)
+        bias_bf = const.tile([P, PACK], BF16)
+
+        def load_batch(b):
+            source = q[b].rearrange("(p j) n -> p j n", j=PACK)
+            for j in range(PACK):
+                nc.sync.dma_start(out=q_rows[b][:, j, :], in_=source[:, j, :])
+
+        load_batch(0)
+        nc.sync.dma_start(out=w_sb[:], in_=Wq.rearrange("(p m) i -> p m i", m=PACK))
+        nc.sync.dma_start(out=bias_bf[:], in_=bq.rearrange("(p m) -> p m", m=PACK))
+        load_batch(1)
+        load_batch(2)
+
+        bias = const.tile([P, PACK], F32)
+        nc.vector.tensor_copy(out=bias[:], in_=bias_bf[:])
+
+        w_words = w_sb[:].bitcast(F32).rearrange("p m (w u) -> p m u w", u=2)
+        w_grouped = const.tile([P, PACK, P, PACK], BF16, align_bytes=64)
+        w_grouped_words = w_grouped[:].bitcast(F32)
+        for half in range(2):
+            w_t = psum_setup.tile([P, 2, 2, P], F32)
+            for m in range(2):
+                for u in range(2):
+                    nc.tensor.transpose(w_t[:, m, u, :], w_words[:, 2 * half + m, u, :], identity[:])
+            nc.scalar.copy(
+                out=w_grouped_words[:, 2 * half : 2 * half + 2, :, :],
+                in_=w_t[:].rearrange("p m u o -> p m o u"),
+            )
+        w_codes = const.tile([P, CHANNELS], U32, align_bytes=64)
+        w_scales = const.tile([P, CHANNELS], U8, align_bytes=64)
+        nc.vector.quantize_mx(
+            out=w_codes[:].bitcast(FP8X4),
+            scales=w_scales[:],
+            in_=w_grouped[:].rearrange("p m o t -> p (m o t)"),
+        )
+
+        for b in range(BATCH):
+            q_sb = q_rows[b]
+
+            stats = batch_pool.tile([P, PACK, STAT_PIECES, STAT_DIM], F32)
+            pieces = q_sb[:].rearrange("p j (s n) -> p j s n", s=STAT_PIECES)
+            for j in range(PACK):
+                for s in range(STAT_PIECES):
+                    nc.vector.bn_stats(out=stats[:, j, s, :], in_=pieces[:, j, s, :])
+            mean_var = batch_pool.tile([P, PACK, 2], F32)
+            for j in range(PACK):
+                nc.vector.bn_aggr(
+                    out=mean_var[:, j, :], in_=stats[:, j, :, :].rearrange("p s d -> p (s d)")
+                )
+            var_eps = batch_pool.tile([P, PACK], F32)
+            nc.vector.tensor_scalar_add(out=var_eps[:], in0=mean_var[:, :, 1], scalar1=EPS)
+            std = batch_pool.tile([P, PACK], F32)
+            nc.scalar.activation(out=std[:], in_=var_eps[:], func=ACT.Sqrt)
+            rstd = batch_pool.tile([P, PACK], F32)
+            nc.vector.reciprocal(out=rstd[:], in_=std[:])
+
+            xn = batch_pool.tile([P, PACK, POSITIONS], BF16)
+            for j in range(PACK):
+                nc.vector.tensor_scalar(
+                    out=xn[:, j, :],
+                    in0=q_sb[:, j, :],
+                    scalar1=mean_var[:, j, 0:1],
+                    scalar2=rstd[:, j : j + 1],
+                    op0=ALU.subtract,
+                    op1=ALU.mult,
+                )
+
+            grouped = batch_pool.tile([P, POSITIONS, PACK], BF16, align_bytes=64)
+            x_codes = batch_pool.tile([P, POSITIONS], U32, align_bytes=64)
+            x_scales = batch_pool.tile([P, POSITIONS], U8, align_bytes=64)
+            for first, width in (NARROW, WIDE):
+                cols = slice(first, first + width)
+                source = xn[:, :, cols].rearrange("p t (c i) -> p c t i", i=4)
+                target = grouped[:, cols, :].rearrange("p (c i) t -> p c t i", i=4)
+                if width == WIDE[1]:
+                    nc.scalar.copy(out=target, in_=source)
+                else:
+                    nc.vector.tensor_copy(out=target, in_=source)
+            for first, width in (NARROW, WIDE):
+                cols = slice(first, first + width)
+                nc.vector.quantize_mx(
+                    out=x_codes[:, cols].bitcast(FP8X4),
+                    scales=x_scales[:, cols],
+                    in_=grouped[:, cols, :].rearrange("p n t -> p (n t)"),
+                )
+
+            out_sb = batch_pool.tile([P, PACK, POSITIONS], F32)
+            out_rows = out[b].rearrange("(p m) n -> p m n", m=PACK)
+            for m in range(PACK):
+                o_cols = slice(m * P, (m + 1) * P)
+                for first, width in (NARROW, WIDE):
+                    cols = slice(first, first + width)
+                    acc = psum_acc.tile([P, BANK], F32)
+                    nc.tensor.matmul_mx(
+                        out=acc[:, :width],
+                        lhsT=w_codes[:, o_cols].bitcast(FP8X4),
+                        lhsT_scale=w_scales[:, o_cols],
+                        rhs=x_codes[:, cols].bitcast(FP8X4),
+                        rhs_scale=x_scales[:, cols],
+                        start=True,
+                        stop=True,
+                    )
+                    nc.scalar.activation(
+                        out=out_sb[:, m, cols],
+                        in_=acc[:, :width],
+                        func=ACT.Identity,
+                        bias=bias[:, m : m + 1],
+                    )
+                nc.sync.dma_start(out=out_rows[:, m, :], in_=out_sb[:, m, :])

@@ -22,6 +22,8 @@ STAT_DIM = 6
 WIDE = (0, 512)
 NARROW = (512, 256)
 BANK = 512
+BANKS = 8
+LAST = BATCH - 1
 
 FLOPS = 2 * BATCH * CHANNELS * CHANNELS * POSITIONS
 
@@ -31,41 +33,140 @@ def tile_adaattn3dstylizer_pa_kernel(tc, q, Wq, bq, out):
     with ExitStack() as ctx:
         const = ctx.enter_context(tc.tile_pool(name="const", bufs=1))
         batch_pool = ctx.enter_context(tc.tile_pool(name="batch", bufs=BATCH))
-        psum_setup = ctx.enter_context(tc.psum_pool(name="psum_setup", bufs=2))
-        psum_acc = ctx.enter_context(tc.psum_pool(name="psum_acc", bufs=6))
+        psum = ctx.enter_context(tc.psum_pool(name="psum", bufs=BANKS))
+        ctx.enter_context(tc.manual_schedule())
 
-        table_warmer = const.tile([P, 1], F32)
-        nc.vector.memset(table_warmer[:], 1.0)
-        nc.scalar.activation(out=table_warmer[:], in_=table_warmer[:], func=ACT.Sqrt)
-        identity = const.tile([P, P], F32)
-        make_identity(nc, identity[:])
-
-        q_rows = []
+        q_rows, stats, mean_var, var_eps, std, rstd = [], [], [], [], [], []
+        xn, grouped, x_codes, x_scales, out_rows = [], [], [], [], []
         for b in range(BATCH):
             q_sb = batch_pool.tile([P, PACK, POSITIONS], BF16)
             q_rows.append(q_sb)
+            stats_sb = batch_pool.tile([P, PACK, STAT_PIECES, STAT_DIM], F32)
+            stats.append(stats_sb)
+            mean_var_sb = batch_pool.tile([P, PACK, 2], F32)
+            mean_var.append(mean_var_sb)
+            var_eps_sb = batch_pool.tile([P, PACK], F32)
+            var_eps.append(var_eps_sb)
+            std_sb = batch_pool.tile([P, PACK], F32)
+            std.append(std_sb)
+            rstd_sb = batch_pool.tile([P, PACK], F32)
+            rstd.append(rstd_sb)
+            xn_sb = batch_pool.tile([P, PACK, POSITIONS], BF16)
+            xn.append(xn_sb)
+            grouped_sb = batch_pool.tile([P, POSITIONS, PACK], BF16, align_bytes=64)
+            grouped.append(grouped_sb)
+            x_codes_sb = batch_pool.tile([P, POSITIONS], U32, align_bytes=64)
+            x_codes.append(x_codes_sb)
+            x_scales_sb = batch_pool.tile([P, POSITIONS], U8, align_bytes=64)
+            x_scales.append(x_scales_sb)
+            out_sb = batch_pool.tile([P, PACK, POSITIONS], F32)
+            out_rows.append(out_sb)
         w_sb = const.tile([P, PACK, CHANNELS], BF16)
+        w_grouped = const.tile([P, PACK, P, PACK], BF16, align_bytes=64)
+        w_codes = const.tile([P, CHANNELS], U32, align_bytes=64)
+        w_scales = const.tile([P, CHANNELS], U8, align_bytes=64)
         bias_bf = const.tile([P, PACK], BF16)
+        bias = const.tile([P, PACK], F32)
+        identity = const.tile([P, P], F32)
+        table_warmer = const.tile([P, 1], F32)
 
         def load_batch(b):
-            source = q[b].rearrange("(p j) n -> p j n", j=PACK)
+            channel_rows = q[b].rearrange("(p j) n -> p j n", j=PACK)
             for j in range(PACK):
-                nc.sync.dma_start(out=q_rows[b][:, j, :], in_=source[:, j, :])
+                nc.sync.dma_start(out=q_rows[b][:, j, :], in_=channel_rows[:, j, :])
 
+        def statistics(b):
+            pieces = q_rows[b][:].rearrange("p j (s n) -> p j s n", s=STAT_PIECES)
+            for j in range(PACK):
+                for s in range(STAT_PIECES):
+                    nc.vector.bn_stats(out=stats[b][:, j, s, :], in_=pieces[:, j, s, :])
+            for j in range(PACK):
+                nc.vector.bn_aggr(
+                    out=mean_var[b][:, j, :], in_=stats[b][:, j, :, :].rearrange("p s d -> p (s d)")
+                )
+            nc.vector.tensor_scalar_add(out=var_eps[b][:], in0=mean_var[b][:, :, 1], scalar1=EPS)
+            nc.scalar.activation(out=std[b][:], in_=var_eps[b][:], func=ACT.Sqrt)
+
+        def normalise(b):
+            nc.vector.reciprocal(out=rstd[b][:], in_=std[b][:])
+            for j in range(PACK):
+                nc.vector.tensor_scalar(
+                    out=xn[b][:, j, :],
+                    in0=q_rows[b][:, j, :],
+                    scalar1=mean_var[b][:, j, 0:1],
+                    scalar2=rstd[b][:, j : j + 1],
+                    op0=ALU.subtract,
+                    op1=ALU.mult,
+                )
+
+        def regroup(copy, b, col_range):
+            cols = slice(col_range[0], col_range[0] + col_range[1])
+            copy(
+                out=grouped[b][:, cols, :].rearrange("p (c i) t -> p c t i", i=4),
+                in_=xn[b][:, :, cols].rearrange("p t (c i) -> p c t i", i=4),
+            )
+
+        def regroup_on_vector(b):
+            regroup(nc.vector.tensor_copy, b, NARROW)
+            if b == LAST:
+                regroup(nc.vector.tensor_copy, b, WIDE)
+
+        def regroup_on_scalar(b):
+            if b != LAST:
+                regroup(nc.scalar.copy, b, WIDE)
+
+        def quantise(b, col_range):
+            cols = slice(col_range[0], col_range[0] + col_range[1])
+            nc.vector.quantize_mx(
+                out=x_codes[b][:, cols].bitcast(FP8X4),
+                scales=x_scales[b][:, cols],
+                in_=grouped[b][:, cols, :].rearrange("p n t -> p (n t)"),
+            )
+
+        def project(b, m, col_range):
+            cols = slice(col_range[0], col_range[0] + col_range[1])
+            o_cols = slice(m * P, (m + 1) * P)
+            acc = psum.tile([P, BANK], F32, tag="bank")
+            nc.tensor.matmul_mx(
+                out=acc[:, : col_range[1]],
+                lhsT=w_codes[:, o_cols].bitcast(FP8X4),
+                lhsT_scale=w_scales[:, o_cols],
+                rhs=x_codes[b][:, cols].bitcast(FP8X4),
+                rhs_scale=x_scales[b][:, cols],
+                start=True,
+                stop=True,
+            )
+            return acc
+
+        def add_bias(b, m, col_range, acc):
+            cols = slice(col_range[0], col_range[0] + col_range[1])
+            if b == LAST and m % 2 == 1:
+                nc.vector.tensor_scalar_add(
+                    out=out_rows[b][:, m, cols], in0=acc[:, : col_range[1]], scalar1=bias[:, m : m + 1]
+                )
+            else:
+                nc.scalar.activation(
+                    out=out_rows[b][:, m, cols],
+                    in_=acc[:, : col_range[1]],
+                    func=ACT.Identity,
+                    bias=bias[:, m : m + 1],
+                )
+
+        nc.vector.memset(table_warmer[:], 1.0)
+        nc.scalar.activation(out=table_warmer[:], in_=table_warmer[:], func=ACT.Sqrt)
+        make_identity(nc, identity[:])
         load_batch(0)
         nc.sync.dma_start(out=w_sb[:], in_=Wq.rearrange("(p m) i -> p m i", m=PACK))
         nc.sync.dma_start(out=bias_bf[:], in_=bq.rearrange("(p m) -> p m", m=PACK))
         load_batch(1)
         load_batch(2)
 
-        bias = const.tile([P, PACK], F32)
-        nc.vector.tensor_copy(out=bias[:], in_=bias_bf[:])
+        statistics(0)
 
         w_words = w_sb[:].bitcast(F32).rearrange("p m (w u) -> p m u w", u=2)
-        w_grouped = const.tile([P, PACK, P, PACK], BF16, align_bytes=64)
         w_grouped_words = w_grouped[:].bitcast(F32)
         for half in range(2):
-            w_t = psum_setup.tile([P, 2, 2, P], F32)
+            w_t = psum.tile([P, 2, 2, P], F32, tag="bank")
             for m in range(2):
                 for u in range(2):
                     nc.tensor.transpose(w_t[:, m, u, :], w_words[:, 2 * half + m, u, :], identity[:])
@@ -73,8 +174,11 @@ def tile_adaattn3dstylizer_pa_kernel(tc, q, Wq, bq, out):
                 out=w_grouped_words[:, 2 * half : 2 * half + 2, :, :],
                 in_=w_t[:].rearrange("p m u o -> p m o u"),
             )
-        w_codes = const.tile([P, CHANNELS], U32, align_bytes=64)
-        w_scales = const.tile([P, CHANNELS], U8, align_bytes=64)
+
+        normalise(0)
+        regroup_on_vector(0)
+        regroup_on_scalar(0)
+        nc.vector.tensor_copy(out=bias[:], in_=bias_bf[:])
         nc.vector.quantize_mx(
             out=w_codes[:].bitcast(FP8X4),
             scales=w_scales[:],
@@ -82,75 +186,19 @@ def tile_adaattn3dstylizer_pa_kernel(tc, q, Wq, bq, out):
         )
 
         for b in range(BATCH):
-            q_sb = q_rows[b]
-
-            stats = batch_pool.tile([P, PACK, STAT_PIECES, STAT_DIM], F32)
-            pieces = q_sb[:].rearrange("p j (s n) -> p j s n", s=STAT_PIECES)
-            for j in range(PACK):
-                for s in range(STAT_PIECES):
-                    nc.vector.bn_stats(out=stats[:, j, s, :], in_=pieces[:, j, s, :])
-            mean_var = batch_pool.tile([P, PACK, 2], F32)
-            for j in range(PACK):
-                nc.vector.bn_aggr(
-                    out=mean_var[:, j, :], in_=stats[:, j, :, :].rearrange("p s d -> p (s d)")
-                )
-            var_eps = batch_pool.tile([P, PACK], F32)
-            nc.vector.tensor_scalar_add(out=var_eps[:], in0=mean_var[:, :, 1], scalar1=EPS)
-            std = batch_pool.tile([P, PACK], F32)
-            nc.scalar.activation(out=std[:], in_=var_eps[:], func=ACT.Sqrt)
-            rstd = batch_pool.tile([P, PACK], F32)
-            nc.vector.reciprocal(out=rstd[:], in_=std[:])
-
-            xn = batch_pool.tile([P, PACK, POSITIONS], BF16)
-            for j in range(PACK):
-                nc.vector.tensor_scalar(
-                    out=xn[:, j, :],
-                    in0=q_sb[:, j, :],
-                    scalar1=mean_var[:, j, 0:1],
-                    scalar2=rstd[:, j : j + 1],
-                    op0=ALU.subtract,
-                    op1=ALU.mult,
-                )
-
-            grouped = batch_pool.tile([P, POSITIONS, PACK], BF16, align_bytes=64)
-            x_codes = batch_pool.tile([P, POSITIONS], U32, align_bytes=64)
-            x_scales = batch_pool.tile([P, POSITIONS], U8, align_bytes=64)
-            for first, width in (NARROW, WIDE):
-                cols = slice(first, first + width)
-                source = xn[:, :, cols].rearrange("p t (c i) -> p c t i", i=4)
-                target = grouped[:, cols, :].rearrange("p (c i) t -> p c t i", i=4)
-                if width == WIDE[1]:
-                    nc.scalar.copy(out=target, in_=source)
-                else:
-                    nc.vector.tensor_copy(out=target, in_=source)
-            for first, width in (NARROW, WIDE):
-                cols = slice(first, first + width)
-                nc.vector.quantize_mx(
-                    out=x_codes[:, cols].bitcast(FP8X4),
-                    scales=x_scales[:, cols],
-                    in_=grouped[:, cols, :].rearrange("p n t -> p (n t)"),
-                )
-
-            out_sb = batch_pool.tile([P, PACK, POSITIONS], F32)
-            out_rows = out[b].rearrange("(p m) n -> p m n", m=PACK)
+            if b != LAST:
+                statistics(b + 1)
+            quantise(b, NARROW)
+            quantise(b, WIDE)
+            if b != LAST:
+                normalise(b + 1)
+                regroup_on_vector(b + 1)
+            narrow_acc = [project(b, m, NARROW) for m in range(PACK)]
+            wide_acc = [project(b, m, WIDE) for m in range(PACK)]
+            stored_rows = out[b].rearrange("(p m) n -> p m n", m=PACK)
             for m in range(PACK):
-                o_cols = slice(m * P, (m + 1) * P)
-                for first, width in (NARROW, WIDE):
-                    cols = slice(first, first + width)
-                    acc = psum_acc.tile([P, BANK], F32)
-                    nc.tensor.matmul_mx(
-                        out=acc[:, :width],
-                        lhsT=w_codes[:, o_cols].bitcast(FP8X4),
-                        lhsT_scale=w_scales[:, o_cols],
-                        rhs=x_codes[:, cols].bitcast(FP8X4),
-                        rhs_scale=x_scales[:, cols],
-                        start=True,
-                        stop=True,
-                    )
-                    nc.scalar.activation(
-                        out=out_sb[:, m, cols],
-                        in_=acc[:, :width],
-                        func=ACT.Identity,
-                        bias=bias[:, m : m + 1],
-                    )
-                nc.sync.dma_start(out=out_rows[:, m, :], in_=out_sb[:, m, :])
+                if m == PACK // 2 and b != LAST:
+                    regroup_on_scalar(b + 1)
+                add_bias(b, m, NARROW, narrow_acc[m])
+                add_bias(b, m, WIDE, wide_acc[m])
+                nc.sync.dma_start(out=stored_rows[:, m, :], in_=out_rows[b][:, m, :])

@@ -99,6 +99,11 @@ def tile_adaattn3dstylizer_pa_kernel(tc, q, Wq, bq, out):
                     op1=ALU.mult,
                 )
 
+        def gpsimd_copy(out, in_):
+            nc.gpsimd.tensor_scalar(
+                out=out, in0=in_, scalar1=1.0, scalar2=0.0, op0=ALU.mult, op1=ALU.add
+            )
+
         def regroup(copy, b, col_range):
             cols = slice(col_range[0], col_range[0] + col_range[1])
             copy(
@@ -106,14 +111,16 @@ def tile_adaattn3dstylizer_pa_kernel(tc, q, Wq, bq, out):
                 in_=xn[b][:, :, cols].rearrange("p t (c i) -> p c t i", i=4),
             )
 
-        def regroup_on_vector(b):
-            regroup(nc.vector.tensor_copy, b, NARROW)
+        def regroup_beside_statistics(b):
             if b == LAST:
+                regroup(nc.vector.tensor_copy, b, NARROW)
                 regroup(nc.vector.tensor_copy, b, WIDE)
+            else:
+                regroup(gpsimd_copy, b, WIDE)
 
         def regroup_on_scalar(b):
             if b != LAST:
-                regroup(nc.scalar.copy, b, WIDE)
+                regroup(nc.scalar.copy, b, NARROW)
 
         def quantise(b, col_range):
             cols = slice(col_range[0], col_range[0] + col_range[1])
@@ -176,23 +183,24 @@ def tile_adaattn3dstylizer_pa_kernel(tc, q, Wq, bq, out):
             )
 
         normalise(0)
-        regroup_on_vector(0)
+        regroup_beside_statistics(0)
         regroup_on_scalar(0)
-        nc.vector.tensor_copy(out=bias[:], in_=bias_bf[:])
-        nc.vector.quantize_mx(
-            out=w_codes[:].bitcast(FP8X4),
-            scales=w_scales[:],
-            in_=w_grouped[:].rearrange("p m o t -> p (m o t)"),
-        )
 
         for b in range(BATCH):
             if b != LAST:
                 statistics(b + 1)
+            if b == 0:
+                nc.vector.tensor_copy(out=bias[:], in_=bias_bf[:])
+                nc.vector.quantize_mx(
+                    out=w_codes[:].bitcast(FP8X4),
+                    scales=w_scales[:],
+                    in_=w_grouped[:].rearrange("p m o t -> p (m o t)"),
+                )
             quantise(b, NARROW)
             quantise(b, WIDE)
             if b != LAST:
                 normalise(b + 1)
-                regroup_on_vector(b + 1)
+                regroup_beside_statistics(b + 1)
             narrow_acc = [project(b, m, NARROW) for m in range(PACK)]
             wide_acc = [project(b, m, WIDE) for m in range(PACK)]
             stored_rows = out[b].rearrange("(p m) n -> p m n", m=PACK)

@@ -36,7 +36,7 @@ def tile_adaattn3dstylizer_pa_kernel(tc, q, Wq, bq, out):
         psum = ctx.enter_context(tc.psum_pool(name="psum", bufs=BANKS))
         ctx.enter_context(tc.manual_schedule())
 
-        q_rows, stats, mean_var, var_eps, std, rstd = [], [], [], [], [], []
+        q_rows, stats, mean_var, var_eps, rstd = [], [], [], [], []
         xn, grouped, x_codes, x_scales, out_rows = [], [], [], [], []
         for b in range(BATCH):
             q_sb = batch_pool.tile([P, PACK, POSITIONS], BF16)
@@ -47,8 +47,6 @@ def tile_adaattn3dstylizer_pa_kernel(tc, q, Wq, bq, out):
             mean_var.append(mean_var_sb)
             var_eps_sb = batch_pool.tile([P, PACK], F32)
             var_eps.append(var_eps_sb)
-            std_sb = batch_pool.tile([P, PACK], F32)
-            std.append(std_sb)
             rstd_sb = batch_pool.tile([P, PACK], F32)
             rstd.append(rstd_sb)
             xn_sb = batch_pool.tile([P, PACK, POSITIONS], BF16)
@@ -84,11 +82,12 @@ def tile_adaattn3dstylizer_pa_kernel(tc, q, Wq, bq, out):
                 nc.vector.bn_aggr(
                     out=mean_var[b][:, j, :], in_=stats[b][:, j, :, :].rearrange("p s d -> p (s d)")
                 )
+
+        def inverse_deviation(b):
             nc.vector.tensor_scalar_add(out=var_eps[b][:], in0=mean_var[b][:, :, 1], scalar1=EPS)
-            nc.scalar.activation(out=std[b][:], in_=var_eps[b][:], func=ACT.Sqrt)
+            nc.scalar.activation(out=rstd[b][:], in_=var_eps[b][:], func=ACT.Abs_reciprocal_sqrt)
 
         def normalise(b):
-            nc.vector.reciprocal(out=rstd[b][:], in_=std[b][:])
             for j in range(PACK):
                 nc.vector.tensor_scalar(
                     out=xn[b][:, j, :],
@@ -160,7 +159,7 @@ def tile_adaattn3dstylizer_pa_kernel(tc, q, Wq, bq, out):
                 )
 
         nc.vector.memset(table_warmer[:], 1.0)
-        nc.scalar.activation(out=table_warmer[:], in_=table_warmer[:], func=ACT.Sqrt)
+        nc.scalar.activation(out=table_warmer[:], in_=table_warmer[:], func=ACT.Abs_reciprocal_sqrt)
         make_identity(nc, identity[:])
         load_batch(0)
         nc.sync.dma_start(out=w_sb[:], in_=Wq.rearrange("(p m) i -> p m i", m=PACK))
@@ -169,6 +168,7 @@ def tile_adaattn3dstylizer_pa_kernel(tc, q, Wq, bq, out):
         load_batch(2)
 
         statistics(0)
+        inverse_deviation(0)
 
         w_words = w_sb[:].bitcast(F32).rearrange("p m (w u) -> p m u w", u=2)
         w_grouped_words = w_grouped[:].bitcast(F32)
@@ -197,6 +197,8 @@ def tile_adaattn3dstylizer_pa_kernel(tc, q, Wq, bq, out):
                     in_=w_grouped[:].rearrange("p m o t -> p (m o t)"),
                 )
             quantise(b, NARROW)
+            if b != LAST:
+                inverse_deviation(b + 1)
             quantise(b, WIDE)
             if b != LAST:
                 normalise(b + 1)

@@ -19,13 +19,18 @@ POSITIONS = 768
 EPS = 1e-5
 STAT_PIECES = 2
 STAT_DIM = 6
-WIDE = (0, 512)
-NARROW = (512, 256)
 BANK = 512
 BANKS = 8
 LAST = BATCH - 1
 
 FLOPS = 2 * BATCH * CHANNELS * CHANNELS * POSITIONS
+
+WIDE = (0, 512)
+NARROW = (512, 256)
+FIRST_HALF = (0, 256)
+SECOND_HALF = (256, 256)
+SCALAR_ROW = 0
+VECTOR_ROWS = (1, 2, 3)
 
 
 def tile_adaattn3dstylizer_pa_kernel(tc, q, Wq, bq, out):
@@ -36,7 +41,7 @@ def tile_adaattn3dstylizer_pa_kernel(tc, q, Wq, bq, out):
         psum = ctx.enter_context(tc.psum_pool(name="psum", bufs=BANKS))
         ctx.enter_context(tc.manual_schedule())
 
-        q_rows, stats, mean_var, var_eps, rstd = [], [], [], [], []
+        q_rows, stats, mean_var, row_sum, row_mean, row_ss, rstd = [], [], [], [], [], [], []
         xn, grouped, x_codes, x_scales, out_rows = [], [], [], [], []
         for b in range(BATCH):
             q_sb = batch_pool.tile([P, PACK, POSITIONS], BF16)
@@ -45,8 +50,12 @@ def tile_adaattn3dstylizer_pa_kernel(tc, q, Wq, bq, out):
             stats.append(stats_sb)
             mean_var_sb = batch_pool.tile([P, PACK, 2], F32)
             mean_var.append(mean_var_sb)
-            var_eps_sb = batch_pool.tile([P, PACK], F32)
-            var_eps.append(var_eps_sb)
+            row_sum_sb = batch_pool.tile([P, 1], F32)
+            row_sum.append(row_sum_sb)
+            row_mean_sb = batch_pool.tile([P, 1], F32)
+            row_mean.append(row_mean_sb)
+            row_ss_sb = batch_pool.tile([P, 1], F32)
+            row_ss.append(row_ss_sb)
             rstd_sb = batch_pool.tile([P, PACK], F32)
             rstd.append(rstd_sb)
             xn_sb = batch_pool.tile([P, PACK, POSITIONS], BF16)
@@ -67,62 +76,73 @@ def tile_adaattn3dstylizer_pa_kernel(tc, q, Wq, bq, out):
         bias = const.tile([P, PACK], F32)
         identity = const.tile([P, P], F32)
         table_warmer = const.tile([P, 1], F32)
+        zero = const.tile([P, 1], F32)
+        eps = const.tile([P, 1], F32)
+        unread = const.tile([P, POSITIONS], BF16)
 
-        def load_batch(b):
+        def span(col_range):
+            return slice(col_range[0], col_range[0] + col_range[1])
+
+        def load_batch(b, row_order):
             channel_rows = q[b].rearrange("(p j) n -> p j n", j=PACK)
-            for j in range(PACK):
+            for j in row_order:
                 nc.sync.dma_start(out=q_rows[b][:, j, :], in_=channel_rows[:, j, :])
 
-        def statistics(b):
+        def vector_statistics(b):
             pieces = q_rows[b][:].rearrange("p j (s n) -> p j s n", s=STAT_PIECES)
-            for j in range(PACK):
+            for j in VECTOR_ROWS:
                 for s in range(STAT_PIECES):
                     nc.vector.bn_stats(out=stats[b][:, j, s, :], in_=pieces[:, j, s, :])
-            for j in range(PACK):
+            for j in VECTOR_ROWS:
                 nc.vector.bn_aggr(
                     out=mean_var[b][:, j, :], in_=stats[b][:, j, :, :].rearrange("p s d -> p (s d)")
                 )
 
+        def scalar_statistics(b):
+            row = q_rows[b][:, SCALAR_ROW, :]
+            nc.scalar.activation(out=unread[:], in_=row, func=ACT.Copy, accum_out=row_sum[b][:])
+            nc.scalar.activation(out=row_mean[b][:], in_=row_sum[b][:], func=ACT.Copy, scale=1.0 / POSITIONS)
+            nc.scalar.activation(
+                out=unread[:], in_=row, func=ACT.Square, scale=-1.0, bias=row_mean[b][:], accum_out=row_ss[b][:]
+            )
+            nc.scalar.activation(
+                out=rstd[b][:, SCALAR_ROW : SCALAR_ROW + 1],
+                in_=row_ss[b][:],
+                func=ACT.Abs_reciprocal_sqrt,
+                scale=1.0 / POSITIONS,
+                bias=eps[:],
+            )
+
         def inverse_deviation(b):
-            nc.vector.tensor_scalar_add(out=var_eps[b][:], in0=mean_var[b][:, :, 1], scalar1=EPS)
-            nc.scalar.activation(out=rstd[b][:], in_=var_eps[b][:], func=ACT.Abs_reciprocal_sqrt)
+            rows = slice(VECTOR_ROWS[0], VECTOR_ROWS[-1] + 1)
+            nc.scalar.activation(
+                out=rstd[b][:, rows], in_=mean_var[b][:, rows, 1], func=ACT.Abs_reciprocal_sqrt, bias=eps[:]
+            )
 
         def normalise(b):
             for j in range(PACK):
+                mean = row_mean[b][:] if j == SCALAR_ROW else mean_var[b][:, j, 0:1]
                 nc.vector.tensor_scalar(
                     out=xn[b][:, j, :],
                     in0=q_rows[b][:, j, :],
-                    scalar1=mean_var[b][:, j, 0:1],
+                    scalar1=mean,
                     scalar2=rstd[b][:, j : j + 1],
                     op0=ALU.subtract,
                     op1=ALU.mult,
                 )
 
         def gpsimd_copy(out, in_):
-            nc.gpsimd.tensor_scalar(
-                out=out, in0=in_, scalar1=1.0, scalar2=0.0, op0=ALU.mult, op1=ALU.add
-            )
+            nc.gpsimd.tensor_scalar(out=out, in0=in_, scalar1=1.0, scalar2=0.0, op0=ALU.mult, op1=ALU.add)
 
         def regroup(copy, b, col_range):
-            cols = slice(col_range[0], col_range[0] + col_range[1])
+            cols = span(col_range)
             copy(
                 out=grouped[b][:, cols, :].rearrange("p (c i) t -> p c t i", i=4),
                 in_=xn[b][:, :, cols].rearrange("p t (c i) -> p c t i", i=4),
             )
 
-        def regroup_beside_statistics(b):
-            if b == LAST:
-                regroup(nc.vector.tensor_copy, b, NARROW)
-                regroup(nc.vector.tensor_copy, b, WIDE)
-            else:
-                regroup(gpsimd_copy, b, WIDE)
-
-        def regroup_on_scalar(b):
-            if b != LAST:
-                regroup(nc.scalar.copy, b, NARROW)
-
         def quantise(b, col_range):
-            cols = slice(col_range[0], col_range[0] + col_range[1])
+            cols = span(col_range)
             nc.vector.quantize_mx(
                 out=x_codes[b][:, cols].bitcast(FP8X4),
                 scales=x_scales[b][:, cols],
@@ -130,7 +150,7 @@ def tile_adaattn3dstylizer_pa_kernel(tc, q, Wq, bq, out):
             )
 
         def project(b, m, col_range):
-            cols = slice(col_range[0], col_range[0] + col_range[1])
+            cols = span(col_range)
             o_cols = slice(m * P, (m + 1) * P)
             acc = psum.tile([P, BANK], F32, tag="bank")
             nc.tensor.matmul_mx(
@@ -144,9 +164,16 @@ def tile_adaattn3dstylizer_pa_kernel(tc, q, Wq, bq, out):
             )
             return acc
 
-        def add_bias(b, m, col_range, acc):
-            cols = slice(col_range[0], col_range[0] + col_range[1])
-            if b == LAST and m % 2 == 1:
+        def project_batch(b):
+            return {
+                NARROW: [project(b, m, NARROW) for m in range(PACK)],
+                WIDE: [project(b, m, WIDE) for m in range(PACK)],
+            }
+
+        def add_bias(engine, b, m, col_range, accs):
+            cols = span(col_range)
+            acc = accs[col_range][m]
+            if engine == "vector":
                 nc.vector.tensor_scalar_add(
                     out=out_rows[b][:, m, cols], in0=acc[:, : col_range[1]], scalar1=bias[:, m : m + 1]
                 )
@@ -158,16 +185,28 @@ def tile_adaattn3dstylizer_pa_kernel(tc, q, Wq, bq, out):
                     bias=bias[:, m : m + 1],
                 )
 
+        def store_row(b, m):
+            stored_rows = out[b].rearrange("(p m) n -> p m n", m=PACK)
+            nc.sync.dma_start(out=stored_rows[:, m, :], in_=out_rows[b][:, m, :])
+
+        def finish_row(engine, b, m, accs):
+            add_bias(engine, b, m, NARROW, accs)
+            add_bias(engine, b, m, WIDE, accs)
+            store_row(b, m)
+
         nc.vector.memset(table_warmer[:], 1.0)
         nc.scalar.activation(out=table_warmer[:], in_=table_warmer[:], func=ACT.Abs_reciprocal_sqrt)
+        nc.vector.memset(zero[:], 0.0)
+        nc.vector.tensor_scalar_add(out=eps[:], in0=zero[:], scalar1=EPS)
         make_identity(nc, identity[:])
-        load_batch(0)
+        load_batch(0, (1, 0, 2, 3))
         nc.sync.dma_start(out=w_sb[:], in_=Wq.rearrange("(p m) i -> p m i", m=PACK))
         nc.sync.dma_start(out=bias_bf[:], in_=bq.rearrange("(p m) -> p m", m=PACK))
-        load_batch(1)
-        load_batch(2)
+        load_batch(1, (0, 1, 2, 3))
+        load_batch(2, (0, 1, 2, 3))
 
-        statistics(0)
+        scalar_statistics(0)
+        vector_statistics(0)
         inverse_deviation(0)
 
         w_words = w_sb[:].bitcast(F32).rearrange("p m (w u) -> p m u w", u=2)
@@ -183,32 +222,53 @@ def tile_adaattn3dstylizer_pa_kernel(tc, q, Wq, bq, out):
             )
 
         normalise(0)
-        regroup_beside_statistics(0)
-        regroup_on_scalar(0)
-
-        for b in range(BATCH):
-            if b != LAST:
-                statistics(b + 1)
-            if b == 0:
-                nc.vector.tensor_copy(out=bias[:], in_=bias_bf[:])
-                nc.vector.quantize_mx(
-                    out=w_codes[:].bitcast(FP8X4),
-                    scales=w_scales[:],
-                    in_=w_grouped[:].rearrange("p m o t -> p (m o t)"),
-                )
-            quantise(b, NARROW)
-            if b != LAST:
-                inverse_deviation(b + 1)
-            quantise(b, WIDE)
-            if b != LAST:
-                normalise(b + 1)
-                regroup_beside_statistics(b + 1)
-            narrow_acc = [project(b, m, NARROW) for m in range(PACK)]
-            wide_acc = [project(b, m, WIDE) for m in range(PACK)]
-            stored_rows = out[b].rearrange("(p m) n -> p m n", m=PACK)
-            for m in range(PACK):
-                if m == PACK // 2 and b != LAST:
-                    regroup_on_scalar(b + 1)
-                add_bias(b, m, NARROW, narrow_acc[m])
-                add_bias(b, m, WIDE, wide_acc[m])
-                nc.sync.dma_start(out=stored_rows[:, m, :], in_=out_rows[b][:, m, :])
+        regroup(gpsimd_copy, 0, WIDE)
+        regroup(nc.scalar.copy, 0, NARROW)
+        scalar_statistics(1)
+        vector_statistics(1)
+        inverse_deviation(1)
+        scalar_statistics(2)
+        nc.vector.tensor_copy(out=bias[:], in_=bias_bf[:])
+        nc.vector.quantize_mx(
+            out=w_codes[:].bitcast(FP8X4),
+            scales=w_scales[:],
+            in_=w_grouped[:].rearrange("p m o t -> p (m o t)"),
+        )
+        quantise(0, NARROW)
+        quantise(0, WIDE)
+        normalise(1)
+        regroup(gpsimd_copy, 1, WIDE)
+        acc0 = project_batch(0)
+        finish_row("scalar", 0, 0, acc0)
+        regroup(nc.scalar.copy, 1, NARROW)
+        finish_row("scalar", 0, 1, acc0)
+        finish_row("scalar", 0, 2, acc0)
+        vector_statistics(2)
+        inverse_deviation(2)
+        finish_row("scalar", 0, 3, acc0)
+        quantise(1, NARROW)
+        quantise(1, WIDE)
+        normalise(2)
+        acc1 = project_batch(1)
+        regroup(gpsimd_copy, 2, FIRST_HALF)
+        regroup(nc.scalar.copy, 2, NARROW)
+        finish_row("vector", 1, 0, acc1)
+        add_bias("vector", 1, 1, NARROW, acc1)
+        quantise(2, NARROW)
+        quantise(2, FIRST_HALF)
+        regroup(nc.vector.tensor_copy, 2, SECOND_HALF)
+        add_bias("scalar", 1, 1, WIDE, acc1)
+        store_row(1, 1)
+        finish_row("scalar", 1, 2, acc1)
+        add_bias("vector", 1, 3, NARROW, acc1)
+        quantise(2, SECOND_HALF)
+        add_bias("vector", 1, 3, WIDE, acc1)
+        store_row(1, 3)
+        acc2 = project_batch(2)
+        for m in range(PACK):
+            add_bias("scalar", 2, m, NARROW, acc2)
+        stored_rows = out[2].rearrange("(p m) n -> p m n", m=PACK)
+        nc.sync.dma_start(out=stored_rows[:, :, span(NARROW)], in_=out_rows[2][:, :, span(NARROW)])
+        for m in range(PACK):
+            add_bias("vector" if m % 2 == 1 else "scalar", 2, m, WIDE, acc2)
+            nc.sync.dma_start(out=stored_rows[:, m, span(WIDE)], in_=out_rows[2][:, m, span(WIDE)])

@@ -136,6 +136,9 @@ def tile_adaattn3dstylizer_pa_kernel(tc, q, Wq, bq, out):
 
         def regroup(copy, b, col_range):
             cols = span(col_range)
+            if copy == gpsimd_copy:
+                copy(out=grouped[b][:, cols, :], in_=xn[b][:, :, cols].rearrange("p t c -> p c t"))
+                return
             copy(
                 out=grouped[b][:, cols, :].rearrange("p (c i) t -> p c t i", i=4),
                 in_=xn[b][:, :, cols].rearrange("p t (c i) -> p c t i", i=4),

@@ -29,6 +29,7 @@ WIDE = (0, 512)
 NARROW = (512, 256)
 FIRST_HALF = (0, 256)
 SECOND_HALF = (256, 256)
+FOLDS = POSITIONS // P
 SCALAR_ROW = 0
 VECTOR_ROWS = (1, 2, 3)
 
@@ -41,7 +42,7 @@ def tile_adaattn3dstylizer_pa_kernel(tc, q, Wq, bq, out):
         psum = ctx.enter_context(tc.psum_pool(name="psum", bufs=BANKS))
         ctx.enter_context(tc.manual_schedule())
 
-        q_rows, stats, mean_var, row_sum, row_mean, row_ss, rstd = [], [], [], [], [], [], []
+        q_rows, stats, mean_var, row_mean, row_ss, rstd = [], [], [], [], [], []
         xn, grouped, x_codes, x_scales, out_rows = [], [], [], [], []
         for b in range(BATCH):
             q_sb = batch_pool.tile([P, PACK, POSITIONS], BF16)
@@ -50,8 +51,6 @@ def tile_adaattn3dstylizer_pa_kernel(tc, q, Wq, bq, out):
             stats.append(stats_sb)
             mean_var_sb = batch_pool.tile([P, PACK, 2], F32)
             mean_var.append(mean_var_sb)
-            row_sum_sb = batch_pool.tile([P, 1], F32)
-            row_sum.append(row_sum_sb)
             row_mean_sb = batch_pool.tile([P, 1], F32)
             row_mean.append(row_mean_sb)
             row_ss_sb = batch_pool.tile([P, 1], F32)
@@ -75,6 +74,7 @@ def tile_adaattn3dstylizer_pa_kernel(tc, q, Wq, bq, out):
         bias_bf = const.tile([P, PACK], BF16)
         bias = const.tile([P, PACK], F32)
         identity = const.tile([P, P], F32)
+        identity_bf = const.tile([P, P], BF16)
         table_warmer = const.tile([P, 1], F32)
         zero = const.tile([P, 1], F32)
         eps = const.tile([P, 1], F32)
@@ -98,10 +98,24 @@ def tile_adaattn3dstylizer_pa_kernel(tc, q, Wq, bq, out):
                     out=mean_var[b][:, j, :], in_=stats[b][:, j, :, :].rearrange("p s d -> p (s d)")
                 )
 
-        def scalar_statistics(b):
+        def fold_row(b):
             row = q_rows[b][:, SCALAR_ROW, :]
-            nc.scalar.activation(out=unread[:], in_=row, func=ACT.Copy, accum_out=row_sum[b][:])
-            nc.scalar.activation(out=row_mean[b][:], in_=row_sum[b][:], func=ACT.Copy, scale=1.0 / POSITIONS)
+            folded = psum.tile([P, BANK], F32, tag="bank")
+            for h in range(FOLDS):
+                nc.tensor.matmul(
+                    out=folded[:, :P],
+                    lhsT=identity_bf[:],
+                    rhs=row[:, h * P : (h + 1) * P],
+                    start=(h == 0),
+                    stop=(h == FOLDS - 1),
+                )
+            return folded
+
+        def scalar_statistics(b, folded):
+            row = q_rows[b][:, SCALAR_ROW, :]
+            nc.scalar.activation(
+                out=unread[:, :P], in_=folded[:, :P], func=ACT.Copy, scale=1.0 / POSITIONS, accum_out=row_mean[b][:]
+            )
             nc.scalar.activation(
                 out=unread[:], in_=row, func=ACT.Square, scale=-1.0, bias=row_mean[b][:], accum_out=row_ss[b][:]
             )
@@ -168,10 +182,11 @@ def tile_adaattn3dstylizer_pa_kernel(tc, q, Wq, bq, out):
             return acc
 
         def project_batch(b):
-            return {
-                NARROW: [project(b, m, NARROW) for m in range(PACK)],
-                WIDE: [project(b, m, WIDE) for m in range(PACK)],
-            }
+            accs = {NARROW: [], WIDE: []}
+            for m in range(PACK):
+                accs[NARROW].append(project(b, m, NARROW))
+                accs[WIDE].append(project(b, m, WIDE))
+            return accs
 
         def add_bias(engine, b, m, col_range, accs):
             cols = span(col_range)
@@ -201,6 +216,7 @@ def tile_adaattn3dstylizer_pa_kernel(tc, q, Wq, bq, out):
         nc.scalar.activation(out=table_warmer[:], in_=table_warmer[:], func=ACT.Abs_reciprocal_sqrt)
         nc.vector.memset(zero[:], 0.0)
         nc.vector.tensor_scalar_add(out=eps[:], in0=zero[:], scalar1=EPS)
+        make_identity(nc, identity_bf[:])
         make_identity(nc, identity[:])
         load_batch(0, (1, 0, 2, 3))
         nc.sync.dma_start(out=w_sb[:], in_=Wq.rearrange("(p m) i -> p m i", m=PACK))
@@ -208,7 +224,7 @@ def tile_adaattn3dstylizer_pa_kernel(tc, q, Wq, bq, out):
         load_batch(1, (0, 1, 2, 3))
         load_batch(2, (0, 1, 2, 3))
 
-        scalar_statistics(0)
+        scalar_statistics(0, fold_row(0))
         vector_statistics(0)
         inverse_deviation(0)
 
@@ -224,13 +240,15 @@ def tile_adaattn3dstylizer_pa_kernel(tc, q, Wq, bq, out):
                 in_=w_t[:].rearrange("p m u o -> p m o u"),
             )
 
+        folded1 = fold_row(1)
+        folded2 = fold_row(2)
         normalise(0)
         regroup(gpsimd_copy, 0, WIDE)
         regroup(nc.scalar.copy, 0, NARROW)
-        scalar_statistics(1)
+        scalar_statistics(1, folded1)
         vector_statistics(1)
         inverse_deviation(1)
-        scalar_statistics(2)
+        scalar_statistics(2, folded2)
         nc.vector.tensor_copy(out=bias[:], in_=bias_bf[:])
         nc.vector.quantize_mx(
             out=w_codes[:].bitcast(FP8X4),
@@ -253,25 +271,25 @@ def tile_adaattn3dstylizer_pa_kernel(tc, q, Wq, bq, out):
         quantise(1, WIDE)
         normalise(2)
         acc1 = project_batch(1)
+        finish_row("scalar", 1, 0, acc1)
         regroup(gpsimd_copy, 2, FIRST_HALF)
         regroup(nc.scalar.copy, 2, NARROW)
-        finish_row("vector", 1, 0, acc1)
-        add_bias("vector", 1, 1, NARROW, acc1)
+        finish_row("vector", 1, 1, acc1)
+        add_bias("vector", 1, 2, NARROW, acc1)
         quantise(2, NARROW)
         quantise(2, FIRST_HALF)
         regroup(nc.vector.tensor_copy, 2, SECOND_HALF)
-        add_bias("scalar", 1, 1, WIDE, acc1)
-        store_row(1, 1)
-        finish_row("scalar", 1, 2, acc1)
-        add_bias("vector", 1, 3, NARROW, acc1)
+        add_bias("scalar", 1, 2, WIDE, acc1)
+        store_row(1, 2)
+        finish_row("scalar", 1, 3, acc1)
+        acc2_narrow = {NARROW: [project(2, m, NARROW) for m in range(PACK)]}
+        add_bias("vector", 2, 0, NARROW, acc2_narrow)
         quantise(2, SECOND_HALF)
-        add_bias("vector", 1, 3, WIDE, acc1)
-        store_row(1, 3)
-        acc2 = project_batch(2)
-        for m in range(PACK):
-            add_bias("scalar", 2, m, NARROW, acc2)
+        acc2_wide = {WIDE: [project(2, m, WIDE) for m in range(PACK)]}
+        for m in range(1, PACK):
+            add_bias("scalar", 2, m, NARROW, acc2_narrow)
         stored_rows = out[2].rearrange("(p m) n -> p m n", m=PACK)
         nc.sync.dma_start(out=stored_rows[:, :, span(NARROW)], in_=out_rows[2][:, :, span(NARROW)])
         for m in range(PACK):
-            add_bias("vector" if m % 2 == 1 else "scalar", 2, m, WIDE, acc2)
+            add_bias("vector" if m % 2 == 1 else "scalar", 2, m, WIDE, acc2_wide)
             nc.sync.dma_start(out=stored_rows[:, m, span(WIDE)], in_=out_rows[2][:, m, span(WIDE)])

@@ -166,10 +166,29 @@ def tile_adaattn3dstylizer_pa_kernel(tc, q, Wq, bq, out):
                 in_=grouped[b][:, cols, :].rearrange("p n t -> p (n t)"),
             )
 
-        def project(b, m, col_range):
+        def warm_banks(b, count):
+            banks = []
+            for i in range(count):
+                acc = psum.tile([P, BANK], F32, tag="bank")
+                nc.tensor.matmul_mx(
+                    out=acc[:],
+                    lhsT=w_codes[:, :P].bitcast(FP8X4),
+                    lhsT_scale=w_scales[:, :P],
+                    rhs=x_codes[b][:, span(WIDE)].bitcast(FP8X4),
+                    rhs_scale=x_scales[b][:, span(WIDE)],
+                    start=True,
+                    stop=True,
+                )
+                banks.append(acc)
+            return banks
+
+        def project(b, m, col_range, warmed):
             cols = span(col_range)
             o_cols = slice(m * P, (m + 1) * P)
-            acc = psum.tile([P, BANK], F32, tag="bank")
+            if warmed:
+                acc = warmed.pop(0)
+            else:
+                acc = psum.tile([P, BANK], F32, tag="bank")
             nc.tensor.matmul_mx(
                 out=acc[:, : col_range[1]],
                 lhsT=w_codes[:, o_cols].bitcast(FP8X4),
@@ -181,11 +200,11 @@ def tile_adaattn3dstylizer_pa_kernel(tc, q, Wq, bq, out):
             )
             return acc
 
-        def project_batch(b):
+        def project_batch(b, warmed):
             accs = {NARROW: [], WIDE: []}
             for m in range(PACK):
-                accs[NARROW].append(project(b, m, NARROW))
-                accs[WIDE].append(project(b, m, WIDE))
+                accs[NARROW].append(project(b, m, NARROW, warmed))
+                accs[WIDE].append(project(b, m, WIDE, warmed))
             return accs
 
         def add_bias(engine, b, m, col_range, accs):
@@ -259,7 +278,8 @@ def tile_adaattn3dstylizer_pa_kernel(tc, q, Wq, bq, out):
         quantise(0, WIDE)
         normalise(1)
         regroup(gpsimd_copy, 1, WIDE)
-        acc0 = project_batch(0)
+        acc0 = project_batch(0, [])
+        warmed1 = warm_banks(0, 4)
         finish_row("scalar", 0, 0, acc0)
         regroup(nc.scalar.copy, 1, NARROW)
         finish_row("scalar", 0, 1, acc0)
@@ -270,7 +290,8 @@ def tile_adaattn3dstylizer_pa_kernel(tc, q, Wq, bq, out):
         quantise(1, NARROW)
         quantise(1, WIDE)
         normalise(2)
-        acc1 = project_batch(1)
+        acc1 = project_batch(1, warmed1)
+        warmed2 = warm_banks(1, 4)
         finish_row("scalar", 1, 0, acc1)
         regroup(gpsimd_copy, 2, FIRST_HALF)
         regroup(nc.scalar.copy, 2, NARROW)
@@ -282,10 +303,11 @@ def tile_adaattn3dstylizer_pa_kernel(tc, q, Wq, bq, out):
         add_bias("scalar", 1, 2, WIDE, acc1)
         store_row(1, 2)
         finish_row("scalar", 1, 3, acc1)
-        acc2_narrow = {NARROW: [project(2, m, NARROW) for m in range(PACK)]}
+        acc2_narrow = {NARROW: [project(2, m, NARROW, warmed2) for m in range(PACK)]}
+        warmed2_wide = warm_banks(1, 1)
         add_bias("vector", 2, 0, NARROW, acc2_narrow)
         quantise(2, SECOND_HALF)
-        acc2_wide = {WIDE: [project(2, m, WIDE) for m in range(PACK)]}
+        acc2_wide = {WIDE: [project(2, m, WIDE, warmed2_wide) for m in range(PACK)]}
         for m in range(1, PACK):
             add_bias("scalar", 2, m, NARROW, acc2_narrow)
         stored_rows = out[2].rearrange("(p m) n -> p m n", m=PACK)

from contextlib import ExitStack

import concourse.mybir as mybir
from concourse.masks import make_identity

F32 = mybir.dt.float32
BF16 = mybir.dt.bfloat16
U32 = mybir.dt.uint32
U8 = mybir.dt.uint8
FP8X4 = mybir.dt.float8_e4m3fn_x4
ALU = mybir.AluOpType
ACT = mybir.ActivationFunctionType

P = 128
PACK = 4
BATCH = 3
CHANNELS = P * PACK
POSITIONS = 768
EPS = 1e-5
STAT_PIECES = 2
STAT_DIM = 6
BANK = 512
BANKS = 8
LAST = BATCH - 1

FLOPS = 2 * BATCH * CHANNELS * CHANNELS * POSITIONS

WIDE = (0, 512)
NARROW = (512, 256)
FIRST_HALF = (0, 256)
SECOND_HALF = (256, 256)
FOLDS = POSITIONS // P
SCALAR_ROW = 0
VECTOR_ROWS = (1, 2, 3)


def tile_adaattn3dstylizer_pa_kernel(tc, q, Wq, bq, out):
    nc = tc.nc
    with ExitStack() as ctx:
        const = ctx.enter_context(tc.tile_pool(name="const", bufs=1))
        batch_pool = ctx.enter_context(tc.tile_pool(name="batch", bufs=BATCH))
        psum = ctx.enter_context(tc.psum_pool(name="psum", bufs=BANKS))
        ctx.enter_context(tc.manual_schedule())

        q_rows, stats, mean_var, row_mean, row_ss, rstd = [], [], [], [], [], []
        xn, grouped, x_codes, x_scales, out_rows = [], [], [], [], []
        for b in range(BATCH):
            q_sb = batch_pool.tile([P, PACK, POSITIONS], BF16)
            q_rows.append(q_sb)
            stats_sb = batch_pool.tile([P, PACK, STAT_PIECES, STAT_DIM], F32)
            stats.append(stats_sb)
            mean_var_sb = batch_pool.tile([P, PACK, 2], F32)
            mean_var.append(mean_var_sb)
            row_mean_sb = batch_pool.tile([P, 1], F32)
            row_mean.append(row_mean_sb)
            row_ss_sb = batch_pool.tile([P, 1], F32)
            row_ss.append(row_ss_sb)
            rstd_sb = batch_pool.tile([P, PACK], F32)
            rstd.append(rstd_sb)
            xn_sb = batch_pool.tile([P, PACK, POSITIONS], BF16)
            xn.append(xn_sb)
            grouped_sb = batch_pool.tile([P, POSITIONS, PACK], BF16, align_bytes=64)
            grouped.append(grouped_sb)
            x_codes_sb = batch_pool.tile([P, POSITIONS], U32, align_bytes=64)
            x_codes.append(x_codes_sb)
            x_scales_sb = batch_pool.tile([P, POSITIONS], U8, align_bytes=64)
            x_scales.append(x_scales_sb)
            out_sb = batch_pool.tile([P, PACK, POSITIONS], F32)
            out_rows.append(out_sb)
        w_sb = const.tile([P, PACK, CHANNELS], BF16)
        w_grouped = const.tile([P, PACK, P, PACK], BF16, align_bytes=64)
        w_codes = const.tile([P, CHANNELS], U32, align_bytes=64)
        w_scales = const.tile([P, CHANNELS], U8, align_bytes=64)
        bias_bf = const.tile([P, PACK], BF16)
        bias = const.tile([P, PACK], F32)
        identity = const.tile([P, P], F32)
        identity_bf = const.tile([P, P], BF16)
        table_warmer = const.tile([P, 1], F32)
        zero = const.tile([P, 1], F32)
        eps = const.tile([P, 1], F32)
        unread = const.tile([P, POSITIONS], BF16)

        def span(col_range):
            return slice(col_range[0], col_range[0] + col_range[1])

        def load_batch(b, row_order):
            channel_rows = q[b].rearrange("(p j) n -> p j n", j=PACK)
            for j in row_order:
                nc.sync.dma_start(out=q_rows[b][:, j, :], in_=channel_rows[:, j, :])

        def vector_statistics(b):
            pieces = q_rows[b][:].rearrange("p j (s n) -> p j s n", s=STAT_PIECES)
            for j in VECTOR_ROWS:
                for s in range(STAT_PIECES):
                    nc.vector.bn_stats(out=stats[b][:, j, s, :], in_=pieces[:, j, s, :])
            for j in VECTOR_ROWS:
                nc.vector.bn_aggr(
                    out=mean_var[b][:, j, :], in_=stats[b][:, j, :, :].rearrange("p s d -> p (s d)")
                )

        def fold_row(b):
            row = q_rows[b][:, SCALAR_ROW, :]
            folded = psum.tile([P, BANK], F32, tag="bank")
            for h in range(FOLDS):
                nc.tensor.matmul(
                    out=folded[:, :P],
                    lhsT=identity_bf[:],
                    rhs=row[:, h * P : (h + 1) * P],
                    start=(h == 0),
                    stop=(h == FOLDS - 1),
                )
            return folded

        def scalar_statistics(b, folded):
            row = q_rows[b][:, SCALAR_ROW, :]
            nc.scalar.activation(
                out=unread[:, :P], in_=folded[:, :P], func=ACT.Copy, scale=1.0 / POSITIONS, accum_out=row_mean[b][:]
            )
            nc.scalar.activation(
                out=unread[:], in_=row, func=ACT.Square, scale=-1.0, bias=row_mean[b][:], accum_out=row_ss[b][:]
            )
            nc.scalar.activation(
                out=rstd[b][:, SCALAR_ROW : SCALAR_ROW + 1],
                in_=row_ss[b][:],
                func=ACT.Abs_reciprocal_sqrt,
                scale=1.0 / POSITIONS,
                bias=eps[:],
            )

        def inverse_deviation(b):
            rows = slice(VECTOR_ROWS[0], VECTOR_ROWS[-1] + 1)
            nc.scalar.activation(
                out=rstd[b][:, rows], in_=mean_var[b][:, rows, 1], func=ACT.Abs_reciprocal_sqrt, bias=eps[:]
            )

        def normalise(b):
            for j in range(PACK):
                mean = row_mean[b][:] if j == SCALAR_ROW else mean_var[b][:, j, 0:1]
                nc.vector.tensor_scalar(
                    out=xn[b][:, j, :],
                    in0=q_rows[b][:, j, :],
                    scalar1=mean,
                    scalar2=rstd[b][:, j : j + 1],
                    op0=ALU.subtract,
                    op1=ALU.mult,
                )

        def gpsimd_copy(out, in_):
            nc.gpsimd.tensor_scalar(out=out, in0=in_, scalar1=1.0, scalar2=0.0, op0=ALU.mult, op1=ALU.add)

        def regroup(copy, b, col_range):
            cols = span(col_range)
            if copy == gpsimd_copy:
                copy(out=grouped[b][:, cols, :], in_=xn[b][:, :, cols].rearrange("p t c -> p c t"))
                return
            copy(
                out=grouped[b][:, cols, :].rearrange("p (c i) t -> p c t i", i=4),
                in_=xn[b][:, :, cols].rearrange("p t (c i) -> p c t i", i=4),
            )

        def quantise(b, col_range):
            cols = span(col_range)
            nc.vector.quantize_mx(
                out=x_codes[b][:, cols].bitcast(FP8X4),
                scales=x_scales[b][:, cols],
                in_=grouped[b][:, cols, :].rearrange("p n t -> p (n t)"),
            )

        def warm_banks(b, count):
            banks = []
            for i in range(count):
                acc = psum.tile([P, BANK], F32, tag="bank")
                nc.tensor.matmul_mx(
                    out=acc[:],
                    lhsT=w_codes[:, :P].bitcast(FP8X4),
                    lhsT_scale=w_scales[:, :P],
                    rhs=x_codes[b][:, span(WIDE)].bitcast(FP8X4),
                    rhs_scale=x_scales[b][:, span(WIDE)],
                    start=True,
                    stop=True,
                )
                banks.append(acc)
            return banks

        def project(b, m, col_range, warmed):
            cols = span(col_range)
            o_cols = slice(m * P, (m + 1) * P)
            if warmed:
                acc = warmed.pop(0)
            else:
                acc = psum.tile([P, BANK], F32, tag="bank")
            nc.tensor.matmul_mx(
                out=acc[:, : col_range[1]],
                lhsT=w_codes[:, o_cols].bitcast(FP8X4),
                lhsT_scale=w_scales[:, o_cols],
                rhs=x_codes[b][:, cols].bitcast(FP8X4),
                rhs_scale=x_scales[b][:, cols],
                start=True,
                stop=True,
            )
            return acc

        def project_batch(b, warmed):
            accs = {NARROW: [], WIDE: []}
            for m in range(PACK):
                accs[NARROW].append(project(b, m, NARROW, warmed))
                accs[WIDE].append(project(b, m, WIDE, warmed))
            return accs

        def add_bias(engine, b, m, col_range, accs):
            cols = span(col_range)
            acc = accs[col_range][m]
            if engine == "vector":
                nc.vector.tensor_scalar_add(
                    out=out_rows[b][:, m, cols], in0=acc[:, : col_range[1]], scalar1=bias[:, m : m + 1]
                )
            else:
                nc.scalar.activation(
                    out=out_rows[b][:, m, cols],
                    in_=acc[:, : col_range[1]],
                    func=ACT.Identity,
                    bias=bias[:, m : m + 1],
                )

        def store_row(b, m):
            stored_rows = out[b].rearrange("(p m) n -> p m n", m=PACK)
            nc.sync.dma_start(out=stored_rows[:, m, :], in_=out_rows[b][:, m, :])

        def finish_row(engine, b, m, accs):
            add_bias(engine, b, m, NARROW, accs)
            add_bias(engine, b, m, WIDE, accs)
            store_row(b, m)

        nc.vector.memset(table_warmer[:], 1.0)
        nc.scalar.activation(out=table_warmer[:], in_=table_warmer[:], func=ACT.Abs_reciprocal_sqrt)
        nc.vector.memset(zero[:], 0.0)
        nc.vector.tensor_scalar_add(out=eps[:], in0=zero[:], scalar1=EPS)
        make_identity(nc, identity_bf[:])
        make_identity(nc, identity[:])
        load_batch(0, (1, 0, 2, 3))
        nc.sync.dma_start(out=w_sb[:], in_=Wq.rearrange("(p m) i -> p m i", m=PACK))
        nc.sync.dma_start(out=bias_bf[:], in_=bq.rearrange("(p m) -> p m", m=PACK))
        load_batch(1, (0, 1, 2, 3))
        load_batch(2, (0, 1, 2, 3))

        scalar_statistics(0, fold_row(0))
        vector_statistics(0)
        inverse_deviation(0)

        w_words = w_sb[:].bitcast(F32).rearrange("p m (w u) -> p m u w", u=2)
        w_grouped_words = w_grouped[:].bitcast(F32)
        for half in range(2):
            w_t = psum.tile([P, 2, 2, P], F32, tag="bank")
            for m in range(2):
                for u in range(2):
                    nc.tensor.transpose(w_t[:, m, u, :], w_words[:, 2 * half + m, u, :], identity[:])
            nc.scalar.copy(
                out=w_grouped_words[:, 2 * half : 2 * half + 2, :, :],
                in_=w_t[:].rearrange("p m u o -> p m o u"),
            )

        folded1 = fold_row(1)
        folded2 = fold_row(2)
        normalise(0)
        regroup(gpsimd_copy, 0, WIDE)
        regroup(nc.scalar.copy, 0, NARROW)
        scalar_statistics(1, folded1)
        vector_statistics(1)
        inverse_deviation(1)
        scalar_statistics(2, folded2)
        nc.vector.tensor_copy(out=bias[:], in_=bias_bf[:])
        nc.vector.quantize_mx(
            out=w_codes[:].bitcast(FP8X4),
            scales=w_scales[:],
            in_=w_grouped[:].rearrange("p m o t -> p (m o t)"),
        )
        quantise(0, NARROW)
        quantise(0, WIDE)
        normalise(1)
        regroup(gpsimd_copy, 1, WIDE)
        acc0 = project_batch(0, [])
        warmed1 = warm_banks(0, 4)
        finish_row("scalar", 0, 0, acc0)
        regroup(nc.scalar.copy, 1, NARROW)
        finish_row("scalar", 0, 1, acc0)
        finish_row("scalar", 0, 2, acc0)
        vector_statistics(2)
        inverse_deviation(2)
        finish_row("scalar", 0, 3, acc0)
        quantise(1, NARROW)
        quantise(1, WIDE)
        normalise(2)
        acc1 = project_batch(1, warmed1)
        warmed2 = warm_banks(1, 4)
        finish_row("scalar", 1, 0, acc1)
        regroup(gpsimd_copy, 2, FIRST_HALF)
        regroup(nc.scalar.copy, 2, NARROW)
        finish_row("vector", 1, 1, acc1)
        add_bias("vector", 1, 2, NARROW, acc1)
        quantise(2, NARROW)
        quantise(2, FIRST_HALF)
        regroup(nc.vector.tensor_copy, 2, SECOND_HALF)
        add_bias("scalar", 1, 2, WIDE, acc1)
        store_row(1, 2)
        finish_row("scalar", 1, 3, acc1)
        acc2_narrow = {NARROW: [project(2, m, NARROW, warmed2) for m in range(PACK)]}
        warmed2_wide = warm_banks(1, 1)
        add_bias("vector", 2, 0, NARROW, acc2_narrow)
        quantise(2, SECOND_HALF)
        acc2_wide = {WIDE: [project(2, m, WIDE, warmed2_wide) for m in range(PACK)]}
        for m in range(1, PACK):
            add_bias("scalar", 2, m, NARROW, acc2_narrow)
        stored_rows = out[2].rearrange("(p m) n -> p m n", m=PACK)
        nc.sync.dma_start(out=stored_rows[:, :, span(NARROW)], in_=out_rows[2][:, :, span(NARROW)])
        for m in range(PACK):
            add_bias("vector" if m % 2 == 1 else "scalar", 2, m, WIDE, acc2_wide)
            nc.sync.dma_start(out=stored_rows[:, m, span(WIDE)], in_=out_rows[2][:, m, span(WIDE)])
